import numpy as np
import ml_dtypes


def mxq(x, axis, fmt="e4m3"):
    dtype, down = {"e4m3": (ml_dtypes.float8_e4m3fn, 7), "e5m2": (ml_dtypes.float8_e5m2, 14)}[fmt]
    v = np.moveaxis(np.asarray(x, np.float32).astype(ml_dtypes.bfloat16).astype(np.float64), axis, -1)
    blocks = v.reshape(v.shape[:-1] + (-1, 32))
    amax = np.abs(blocks).max(-1, keepdims=True)
    byte = np.maximum(np.where(amax > 0, np.frexp(amax)[1] - 1 + 127, 0) - down, 1)
    scale = np.exp2(byte - 127.0)
    codes = (blocks / scale).astype(np.float32).astype(dtype).astype(np.float64)
    return np.moveaxis((codes * scale).reshape(v.shape), -1, axis)


WIDE = False


def mx_kscale(k):
    if not WIDE:
        return np.ones(k)
    levels = np.array([10, -10, 5, -5, 0])
    a = np.random.permutation(np.resize(levels, k // 512 * 4)).reshape(k // 512, 4)
    idx = np.arange(k)
    return np.exp2(a[idx // 512, idx % 128 // 32])


BF16 = ml_dtypes.bfloat16


def bf(x):
    return np.asarray(x, np.float32).astype(BF16)


def f64(x):
    return np.asarray(x).astype(np.float64)


B, N, DI, D, H, DO = 8, 1024, 512, 256, 4, 1024
DH = D // H
SIG = 0.5


def time_concat(space):
    t = np.sqrt(1.0 + np.sum(space * space, axis=-1, keepdims=True))
    return np.concatenate([t, space], axis=-1)


def split_lift(space):
    return time_concat(space.reshape(B, N, H, DH).transpose(0, 2, 1, 3))


def setup_inputs():
    s = mx_kscale(DI)
    return {"x_space": bf(np.random.standard_normal((B, N, DI)) * s),
            "Wq": bf(np.random.standard_normal((D, DI)) * SIG / np.sqrt(DI) / s),
            "bq": bf(np.random.standard_normal(D) * 0.1),
            "Wk": bf(np.random.standard_normal((D, DI)) * SIG / np.sqrt(DI) / s),
            "bk": bf(np.random.standard_normal(D) * 0.1)}


def reference(x_space, Wq, bq, Wk, bk):
    xq = mxq(f64(x_space), 2, "e4m3")
    q = (xq @ mxq(f64(Wq), 1, "e4m3").T) + f64(bq)
    k = (xq @ mxq(f64(Wk), 1, "e4m3").T) + f64(bk)
    return split_lift(q), split_lift(k)

@@ -1,0 +1,210 @@
+from contextlib import ExitStack
+
+import concourse.mybir as mybir
+from concourse.masks import make_identity
+
+F32 = mybir.dt.float32
+BF16 = mybir.dt.bfloat16
+U32 = mybir.dt.uint32
+U8 = mybir.dt.uint8
+FP8X4 = mybir.dt.float8_e4m3fn_x4
+ADD = mybir.AluOpType.add
+SQUARE = mybir.ActivationFunctionType.Square
+SQRT = mybir.ActivationFunctionType.Sqrt
+
+P = 128
+BATCHES = 8
+TOKENS = 1024
+K = 512
+WORDS = K // 2
+FEATURES = 512
+HEAD = 64
+ROW = HEAD + 1
+TILES = TOKENS // P
+HALF = TILES // 2
+PIECE_HEADS = P // HEAD
+PIECE_ROWS = PIECE_HEADS * TILES
+PIECES_PER_BATCH = FEATURES // P
+PIECES = BATCHES * PIECES_PER_BATCH
+PAIRS = BATCHES * TILES // 2
+
+LAG_QUANTISE = 1
+LAG_PROJECT = 5
+LAG_SQUARE = LAG_PROJECT + 1
+LAG_REDUCE = LAG_SQUARE + 1
+LAG_ROOT = LAG_REDUCE + 1
+
+FLOPS = 2 * BATCHES * TOKENS * K * FEATURES
+
+
+def turn_two_tiles(nc, banks, identity, raw_words, grouped_words):
+    bank = banks.tile([P, 4 * P], F32)
+    for i in range(2):
+        for u in range(2):
+            nc.tensor.transpose(
+                bank[:, (2 * i + u) * P : (2 * i + u + 1) * P],
+                raw_words[:, i * WORDS + u * P : i * WORDS + (u + 1) * P],
+                identity,
+            )
+    nc.scalar.copy(
+        out=grouped_words.rearrange("p (i r u) -> p i r u", i=2, u=2),
+        in_=bank[:].rearrange("p (i u r) -> p i r u", i=2, u=2),
+    )
+
+
+def tile_lorentzmultiheadattention_pa_t_kernel(tc, x_space, Wq, bq, Wk, bk, out_0, out_1):
+    nc = tc.nc
+    with ExitStack() as stack:
+        stack.enter_context(tc.manual_schedule())
+        const = stack.enter_context(tc.tile_pool(name="const", bufs=1))
+        x_pool = stack.enter_context(tc.tile_pool(name="x", bufs=BATCHES))
+        mx_pool = stack.enter_context(tc.tile_pool(name="mx", bufs=4))
+        out_pool = stack.enter_context(tc.tile_pool(name="lifted", bufs=8))
+        sum_pool = stack.enter_context(tc.tile_pool(name="sums", bufs=3))
+        turn_banks = stack.enter_context(tc.psum_pool(name="turned", bufs=4))
+        product_banks = stack.enter_context(tc.psum_pool(name="products", bufs=4))
+
+        w_raw = const.tile([P, 4 * K], BF16)
+        nc.sync.dma_start(
+            out=w_raw[:, 0 : 2 * K].rearrange("p (c k) -> p c k", c=2), in_=Wq.rearrange("(c p) k -> p c k", p=P)
+        )
+        nc.sync.dma_start(
+            out=w_raw[:, 2 * K : 4 * K].rearrange("p (c k) -> p c k", c=2), in_=Wk.rearrange("(c p) k -> p c k", p=P)
+        )
+        x_words = []
+        for b in range(BATCHES):
+            x_raw = x_pool.tile([P, TILES * K], BF16)
+            nc.sync.dma_start(out=x_raw[:], in_=x_space[b].rearrange("(p t) k -> p (t k)", t=TILES))
+            x_words.append(x_raw[:].bitcast(F32))
+
+        identity = const.tile([P, P], F32)
+        make_identity(nc, identity[:])
+        one = const.tile([P, 1], F32)
+        nc.vector.memset(one[:], 1.0)
+        warm = const.tile([P, 1], F32)
+        nc.scalar.activation(out=warm[:], in_=one[:], func=SQRT)
+
+        bias_rows = const.tile([P, FEATURES], BF16)
+        nc.vector.memset(bias_rows[:], 0.0)
+        ones = const.tile([P, P], BF16)
+        nc.vector.memset(ones[:], 1.0)
+        nc.scalar.dma_start(out=bias_rows[0:1, 0 : FEATURES // 2], in_=bq.unsqueeze(0))
+        nc.scalar.dma_start(out=bias_rows[0:1, FEATURES // 2 : FEATURES], in_=bk.unsqueeze(0))
+
+        w_grouped = const.tile([P, 4 * FEATURES], BF16, align_bytes=64)
+        w_codes = const.tile([P, FEATURES], U32, align_bytes=64)
+        w_scales = const.tile([P, FEATURES], U8, align_bytes=64)
+        for j in range(2):
+            turn_two_tiles(
+                nc,
+                turn_banks,
+                identity[:],
+                w_raw[:].bitcast(F32)[:, 2 * j * WORDS : 2 * (j + 1) * WORDS],
+                w_grouped[:].bitcast(F32)[:, 4 * j * P : 4 * (j + 1) * P],
+            )
+        bias_bank = product_banks.tile([P, FEATURES], F32, tag="product")
+        nc.tensor.matmul(out=bias_bank[:], lhsT=ones[:], rhs=bias_rows[:], start=True, stop=True)
+        bias = const.tile([P, FEATURES], F32)
+        nc.vector.tensor_copy(out=bias[:], in_=bias_bank[:])
+        nc.vector.quantize_mx(out=w_codes[:].bitcast(FP8X4), scales=w_scales[:], in_=w_grouped[:])
+
+        grouped = {}
+        codes = {}
+        scales = {}
+        lifted = {}
+        halves = {}
+        norms = {}
+
+        def turn_pair(pair):
+            half_batch, second = divmod(pair, 2)
+            if not second:
+                x_grouped = mx_pool.tile([P, 4 * HALF * P], BF16, align_bytes=64)
+                grouped[half_batch] = x_grouped
+            b, j = divmod(pair, TILES // 2)
+            turn_two_tiles(
+                nc,
+                turn_banks,
+                identity[:],
+                x_words[b][:, 2 * j * WORDS : 2 * (j + 1) * WORDS],
+                grouped[half_batch][:].bitcast(F32)[:, 4 * second * P : 4 * (second + 1) * P],
+            )
+
+        def quantise(half_batch):
+            x_codes = mx_pool.tile([P, HALF * P], U32, align_bytes=64)
+            x_scales = mx_pool.tile([P, HALF * P], U8, align_bytes=64)
+            nc.vector.quantize_mx(out=x_codes[:].bitcast(FP8X4), scales=x_scales[:], in_=grouped[half_batch][:])
+            codes[half_batch] = x_codes
+            scales[half_batch] = x_scales
+
+        def project(piece):
+            b, c = divmod(piece, PIECES_PER_BATCH)
+            features = slice(c * P, (c + 1) * P)
+            rows = out_pool.tile([P, PIECE_ROWS, ROW], F32)
+            lifted[piece] = rows
+            u_by_tile = rows[:, :, 1:ROW].rearrange("p (h t) d -> p t h d", h=PIECE_HEADS)
+            bias_by_tile = (
+                bias[:, features]
+                .rearrange("p (h d) -> p h d", h=PIECE_HEADS)
+                .unsqueeze(1)
+                .to_broadcast([P, HALF, PIECE_HEADS, HEAD])
+            )
+            for half in range(2):
+                half_batch = 2 * b + half
+                product = product_banks.tile([P, HALF * P], F32)
+                for i in range(HALF):
+                    tokens = slice(i * P, (i + 1) * P)
+                    nc.tensor.matmul_mx(
+                        out=product[:, tokens],
+                        lhsT=codes[half_batch][:, tokens].bitcast(FP8X4),
+                        lhsT_scale=scales[half_batch][:, tokens],
+                        rhs=w_codes[:, features].bitcast(FP8X4),
+                        rhs_scale=w_scales[:, features],
+                        start=True,
+                        stop=True,
+                    )
+                nc.vector.tensor_tensor(
+                    out=u_by_tile[:, half * HALF : (half + 1) * HALF],
+                    in0=product[:].rearrange("p (t h d) -> p t h d", t=HALF, h=PIECE_HEADS),
+                    in1=bias_by_tile,
+                    op=ADD,
+                )
+
+        def square(piece):
+            squares = sum_pool.tile([P, PIECE_ROWS, HEAD], F32)
+            nc.scalar.activation(out=squares[:], in_=lifted[piece][:, :, 1:ROW], func=SQUARE)
+            half_sums = sum_pool.tile([P, PIECE_ROWS, HEAD // 2], F32)
+            nc.gpsimd.tensor_tensor(
+                out=half_sums[:], in0=squares[:, :, 0 : HEAD // 2], in1=squares[:, :, HEAD // 2 : HEAD], op=ADD
+            )
+            halves[piece] = half_sums
+
+        def reduce_rows(piece):
+            norm = sum_pool.tile([P, PIECE_ROWS], F32)
+            nc.vector.tensor_reduce(out=norm[:], in_=halves[piece][:], axis=mybir.AxisListType.X, op=ADD)
+            norms[piece] = norm
+
+        def root_and_store(piece):
+            b, c = divmod(piece, PIECES_PER_BATCH)
+            rows = lifted[piece]
+            nc.scalar.activation(out=rows[:, :, 0], in_=norms[piece][:], func=SQRT, bias=one[:])
+            target = (out_0, out_1)[c // 2]
+            first_head = PIECE_HEADS * (c % 2)
+            nc.sync.dma_start(
+                out=target[b, first_head : first_head + PIECE_HEADS].rearrange("h (p t) d -> p h (t d)", t=TILES),
+                in_=rows[:].rearrange("p (h t) d -> p h (t d)", h=PIECE_HEADS),
+            )
+
+        for step in range(PIECES + LAG_ROOT):
+            half_batch, first_pair_only = divmod(step - LAG_QUANTISE - 1, 2)
+            if not first_pair_only and 0 <= half_batch < PAIRS // 2:
+                quantise(half_batch)
+            if 0 <= step - LAG_PROJECT < PIECES:
+                project(step - LAG_PROJECT)
+            if 0 <= step - LAG_SQUARE < PIECES:
+                square(step - LAG_SQUARE)
+            if step < PAIRS:
+                turn_pair(step)
+            if 0 <= step - LAG_REDUCE < PIECES:
+                reduce_rows(step - LAG_REDUCE)
+            if 0 <= step - LAG_ROOT < PIECES:
+                root_and_store(step - LAG_ROOT)

@@ -31,8 +31,10 @@ PAIRS = BATCHES * TILES // 2
 LAG_QUANTISE = 1
 LAG_PROJECT = 5
 LAG_SQUARE = LAG_PROJECT + 1
-LAG_REDUCE = LAG_SQUARE + 1
+LAG_REDUCE = LAG_SQUARE + 2
 LAG_ROOT = LAG_REDUCE + 1
+
+SECOND_HALVING_EVERY = 2
 
 FLOPS = 2 * BATCHES * TOKENS * K * FEATURES
 
@@ -57,10 +59,10 @@ def tile_lorentzmultiheadattention_pa_t_kernel(tc, x_space, Wq, bq, Wk, bk, out_
     with ExitStack() as stack:
         stack.enter_context(tc.manual_schedule())
         const = stack.enter_context(tc.tile_pool(name="const", bufs=1))
-        x_pool = stack.enter_context(tc.tile_pool(name="x", bufs=BATCHES))
+        x_pool = stack.enter_context(tc.tile_pool(name="x", bufs=2 * BATCHES))
         mx_pool = stack.enter_context(tc.tile_pool(name="mx", bufs=4))
         out_pool = stack.enter_context(tc.tile_pool(name="lifted", bufs=8))
-        sum_pool = stack.enter_context(tc.tile_pool(name="sums", bufs=3))
+        sum_pool = stack.enter_context(tc.tile_pool(name="sums", bufs=4))
         turn_banks = stack.enter_context(tc.psum_pool(name="turned", bufs=4))
         product_banks = stack.enter_context(tc.psum_pool(name="products", bufs=4))
 
@@ -73,9 +75,11 @@ def tile_lorentzmultiheadattention_pa_t_kernel(tc, x_space, Wq, bq, Wk, bk, out_
         )
         x_words = []
         for b in range(BATCHES):
-            x_raw = x_pool.tile([P, TILES * K], BF16)
-            nc.sync.dma_start(out=x_raw[:], in_=x_space[b].rearrange("(p t) k -> p (t k)", t=TILES))
-            x_words.append(x_raw[:].bitcast(F32))
+            x_by_tile = x_space[b].rearrange("(p t) k -> p t k", t=TILES)
+            for half in range(2):
+                x_raw = x_pool.tile([P, HALF, K], BF16)
+                nc.sync.dma_start(out=x_raw[:], in_=x_by_tile[:, half * HALF : (half + 1) * HALF, :])
+                x_words.append(x_raw[:].rearrange("p t k -> p (t k)").bitcast(F32))
 
         identity = const.tile([P, P], F32)
         make_identity(nc, identity[:])
@@ -112,7 +116,7 @@ def tile_lorentzmultiheadattention_pa_t_kernel(tc, x_space, Wq, bq, Wk, bk, out_
         codes = {}
         scales = {}
         lifted = {}
-        halves = {}
+        partial_sums = {}
         norms = {}
 
         def turn_pair(pair):
@@ -120,12 +124,11 @@ def tile_lorentzmultiheadattention_pa_t_kernel(tc, x_space, Wq, bq, Wk, bk, out_
             if not second:
                 x_grouped = mx_pool.tile([P, 4 * HALF * P], BF16, align_bytes=64)
                 grouped[half_batch] = x_grouped
-            b, j = divmod(pair, TILES // 2)
             turn_two_tiles(
                 nc,
                 turn_banks,
                 identity[:],
-                x_words[b][:, 2 * j * WORDS : 2 * (j + 1) * WORDS],
+                x_words[half_batch][:, 2 * second * WORDS : 2 * (second + 1) * WORDS],
                 grouped[half_batch][:].bitcast(F32)[:, 4 * second * P : 4 * (second + 1) * P],
             )
 
@@ -176,11 +179,20 @@ def tile_lorentzmultiheadattention_pa_t_kernel(tc, x_space, Wq, bq, Wk, bk, out_
             nc.gpsimd.tensor_tensor(
                 out=half_sums[:], in0=squares[:, :, 0 : HEAD // 2], in1=squares[:, :, HEAD // 2 : HEAD], op=ADD
             )
-            halves[piece] = half_sums
+            partial_sums[piece] = half_sums
+            if piece % SECOND_HALVING_EVERY == 0:
+                quarter_sums = sum_pool.tile([P, PIECE_ROWS, HEAD // 4], F32)
+                nc.gpsimd.tensor_tensor(
+                    out=quarter_sums[:],
+                    in0=half_sums[:, :, 0 : HEAD // 4],
+                    in1=half_sums[:, :, HEAD // 4 : HEAD // 2],
+                    op=ADD,
+                )
+                partial_sums[piece] = quarter_sums
 
         def reduce_rows(piece):
             norm = sum_pool.tile([P, PIECE_ROWS], F32)
-            nc.vector.tensor_reduce(out=norm[:], in_=halves[piece][:], axis=mybir.AxisListType.X, op=ADD)
+            nc.vector.tensor_reduce(out=norm[:], in_=partial_sums[piece][:], axis=mybir.AxisListType.X, op=ADD)
             norms[piece] = norm
 
         def root_and_store(piece):

@@ -26,12 +26,13 @@ PIECE_HEADS = P // HEAD
 PIECE_ROWS = PIECE_HEADS * TILES
 PIECES_PER_BATCH = FEATURES // P
 PIECES = BATCHES * PIECES_PER_BATCH
-PAIRS = BATCHES * TILES // 2
+HALF_BATCHES = 2 * BATCHES
+ROUND_PIECES = PIECES // HALF_BATCHES
 
 LAG_QUANTISE = 1
-LAG_PROJECT = 5
+LAG_PROJECT = 3
 LAG_SQUARE = LAG_PROJECT + 1
-LAG_REDUCE = LAG_SQUARE + 2
+LAG_REDUCE = LAG_SQUARE + 1
 LAG_ROOT = LAG_REDUCE + 1
 
 SECOND_HALVING_EVERY = 2
@@ -61,7 +62,7 @@ def tile_lorentzmultiheadattention_pa_t_kernel(tc, x_space, Wq, bq, Wk, bk, out_
         const = stack.enter_context(tc.tile_pool(name="const", bufs=1))
         x_pool = stack.enter_context(tc.tile_pool(name="x", bufs=2 * BATCHES))
         mx_pool = stack.enter_context(tc.tile_pool(name="mx", bufs=4))
-        out_pool = stack.enter_context(tc.tile_pool(name="lifted", bufs=8))
+        out_pool = stack.enter_context(tc.tile_pool(name="lifted", bufs=12))
         sum_pool = stack.enter_context(tc.tile_pool(name="sums", bufs=4))
         turn_banks = stack.enter_context(tc.psum_pool(name="turned", bufs=4))
         product_banks = stack.enter_context(tc.psum_pool(name="products", bufs=4))
@@ -119,18 +120,17 @@ def tile_lorentzmultiheadattention_pa_t_kernel(tc, x_space, Wq, bq, Wk, bk, out_
         partial_sums = {}
         norms = {}
 
-        def turn_pair(pair):
-            half_batch, second = divmod(pair, 2)
-            if not second:
-                x_grouped = mx_pool.tile([P, 4 * HALF * P], BF16, align_bytes=64)
-                grouped[half_batch] = x_grouped
-            turn_two_tiles(
-                nc,
-                turn_banks,
-                identity[:],
-                x_words[half_batch][:, 2 * second * WORDS : 2 * (second + 1) * WORDS],
-                grouped[half_batch][:].bitcast(F32)[:, 4 * second * P : 4 * (second + 1) * P],
-            )
+        def turn(half_batch):
+            x_grouped = mx_pool.tile([P, 4 * HALF * P], BF16, align_bytes=64)
+            grouped[half_batch] = x_grouped
+            for j in range(HALF // 2):
+                turn_two_tiles(
+                    nc,
+                    turn_banks,
+                    identity[:],
+                    x_words[half_batch][:, 2 * j * WORDS : 2 * (j + 1) * WORDS],
+                    x_grouped[:].bitcast(F32)[:, 4 * j * P : 4 * (j + 1) * P],
+                )
 
         def quantise(half_batch):
             x_codes = mx_pool.tile([P, HALF * P], U32, align_bytes=64)
@@ -206,17 +206,21 @@ def tile_lorentzmultiheadattention_pa_t_kernel(tc, x_space, Wq, bq, Wk, bk, out_
                 in_=rows[:].rearrange("p (h t) d -> p h (t d)", h=PIECE_HEADS),
             )
 
-        for step in range(PIECES + LAG_ROOT):
-            half_batch, first_pair_only = divmod(step - LAG_QUANTISE - 1, 2)
-            if not first_pair_only and 0 <= half_batch < PAIRS // 2:
-                quantise(half_batch)
-            if 0 <= step - LAG_PROJECT < PIECES:
-                project(step - LAG_PROJECT)
-            if 0 <= step - LAG_SQUARE < PIECES:
-                square(step - LAG_SQUARE)
-            if step < PAIRS:
-                turn_pair(step)
-            if 0 <= step - LAG_REDUCE < PIECES:
-                reduce_rows(step - LAG_REDUCE)
-            if 0 <= step - LAG_ROOT < PIECES:
-                root_and_store(step - LAG_ROOT)
+        def pieces_of(r):
+            if 0 <= r < HALF_BATCHES:
+                return range(ROUND_PIECES * r, ROUND_PIECES * (r + 1))
+            return range(0)
+
+        for r in range(HALF_BATCHES + LAG_ROOT):
+            if 0 <= r - LAG_QUANTISE < HALF_BATCHES:
+                quantise(r - LAG_QUANTISE)
+            for piece in pieces_of(r - LAG_PROJECT):
+                project(piece)
+            for piece in pieces_of(r - LAG_SQUARE):
+                square(piece)
+            if r < HALF_BATCHES:
+                turn(r)
+            for piece in pieces_of(r - LAG_REDUCE):
+                reduce_rows(piece)
+            for piece in pieces_of(r - LAG_ROOT):
+                root_and_store(piece)

@@ -40,7 +40,7 @@ SECOND_HALVING_EVERY = 2
 FLOPS = 2 * BATCHES * TOKENS * K * FEATURES
 
 
-def turn_two_tiles(nc, banks, identity, raw_words, grouped_words):
+def transpose_two_tiles(nc, banks, identity, raw_words):
     bank = banks.tile([P, 4 * P], F32)
     for i in range(2):
         for u in range(2):
@@ -49,7 +49,11 @@ def turn_two_tiles(nc, banks, identity, raw_words, grouped_words):
                 raw_words[:, i * WORDS + u * P : i * WORDS + (u + 1) * P],
                 identity,
             )
-    nc.scalar.copy(
+    return bank
+
+
+def regroup_two_tiles(copy, bank, grouped_words):
+    copy(
         out=grouped_words.rearrange("p (i r u) -> p i r u", i=2, u=2),
         in_=bank[:].rearrange("p (i u r) -> p i r u", i=2, u=2),
     )
@@ -100,19 +104,17 @@ def tile_lorentzmultiheadattention_pa_t_kernel(tc, x_space, Wq, bq, Wk, bk, out_
         w_codes = const.tile([P, FEATURES], U32, align_bytes=64)
         w_scales = const.tile([P, FEATURES], U8, align_bytes=64)
         for j in range(2):
-            turn_two_tiles(
-                nc,
-                turn_banks,
-                identity[:],
-                w_raw[:].bitcast(F32)[:, 2 * j * WORDS : 2 * (j + 1) * WORDS],
-                w_grouped[:].bitcast(F32)[:, 4 * j * P : 4 * (j + 1) * P],
+            w_bank = transpose_two_tiles(
+                nc, turn_banks, identity[:], w_raw[:].bitcast(F32)[:, 2 * j * WORDS : 2 * (j + 1) * WORDS]
             )
+            regroup_two_tiles(nc.vector.tensor_copy, w_bank, w_grouped[:].bitcast(F32)[:, 4 * j * P : 4 * (j + 1) * P])
         bias_bank = product_banks.tile([P, FEATURES], F32, tag="product")
         nc.tensor.matmul(out=bias_bank[:], lhsT=ones[:], rhs=bias_rows[:], start=True, stop=True)
         bias = const.tile([P, FEATURES], F32)
         nc.vector.tensor_copy(out=bias[:], in_=bias_bank[:])
         nc.vector.quantize_mx(out=w_codes[:].bitcast(FP8X4), scales=w_scales[:], in_=w_grouped[:])
 
+        turned = {}
         grouped = {}
         codes = {}
         scales = {}
@@ -120,16 +122,21 @@ def tile_lorentzmultiheadattention_pa_t_kernel(tc, x_space, Wq, bq, Wk, bk, out_
         partial_sums = {}
         norms = {}
 
-        def turn(half_batch):
+        def transpose_batch(b):
+            for half_batch in (2 * b, 2 * b + 1):
+                turned[half_batch] = [
+                    transpose_two_tiles(
+                        nc, turn_banks, identity[:], x_words[half_batch][:, 2 * j * WORDS : 2 * (j + 1) * WORDS]
+                    )
+                    for j in range(HALF // 2)
+                ]
+
+        def regroup(half_batch):
             x_grouped = mx_pool.tile([P, 4 * HALF * P], BF16, align_bytes=64)
             grouped[half_batch] = x_grouped
             for j in range(HALF // 2):
-                turn_two_tiles(
-                    nc,
-                    turn_banks,
-                    identity[:],
-                    x_words[half_batch][:, 2 * j * WORDS : 2 * (j + 1) * WORDS],
-                    x_grouped[:].bitcast(F32)[:, 4 * j * P : 4 * (j + 1) * P],
+                regroup_two_tiles(
+                    nc.scalar.copy, turned[half_batch][j], x_grouped[:].bitcast(F32)[:, 4 * j * P : 4 * (j + 1) * P]
                 )
 
         def quantise(half_batch):
@@ -212,14 +219,16 @@ def tile_lorentzmultiheadattention_pa_t_kernel(tc, x_space, Wq, bq, Wk, bk, out_
             return range(0)
 
         for r in range(HALF_BATCHES + LAG_ROOT):
-            if 0 <= r - LAG_QUANTISE < HALF_BATCHES:
-                quantise(r - LAG_QUANTISE)
             for piece in pieces_of(r - LAG_PROJECT):
                 project(piece)
+            if 0 <= r - LAG_QUANTISE < HALF_BATCHES:
+                quantise(r - LAG_QUANTISE)
             for piece in pieces_of(r - LAG_SQUARE):
                 square(piece)
+            if r < HALF_BATCHES and r % 2 == 0:
+                transpose_batch(r // 2)
             if r < HALF_BATCHES:
-                turn(r)
+                regroup(r)
             for piece in pieces_of(r - LAG_REDUCE):
                 reduce_rows(piece)
             for piece in pieces_of(r - LAG_ROOT):

@@ -40,7 +40,7 @@ SECOND_HALVING_EVERY = 2
 FLOPS = 2 * BATCHES * TOKENS * K * FEATURES
 
 
-def transpose_two_tiles(nc, banks, identity, raw_words):
+def turn_two_tiles(nc, banks, identity, raw_words, grouped_words):
     bank = banks.tile([P, 4 * P], F32)
     for i in range(2):
         for u in range(2):
@@ -49,11 +49,7 @@ def transpose_two_tiles(nc, banks, identity, raw_words):
                 raw_words[:, i * WORDS + u * P : i * WORDS + (u + 1) * P],
                 identity,
             )
-    return bank
-
-
-def regroup_two_tiles(copy, bank, grouped_words):
-    copy(
+    nc.scalar.copy(
         out=grouped_words.rearrange("p (i r u) -> p i r u", i=2, u=2),
         in_=bank[:].rearrange("p (i u r) -> p i r u", i=2, u=2),
     )
@@ -71,6 +67,9 @@ def tile_lorentzmultiheadattention_pa_t_kernel(tc, x_space, Wq, bq, Wk, bk, out_
         turn_banks = stack.enter_context(tc.psum_pool(name="turned", bufs=4))
         product_banks = stack.enter_context(tc.psum_pool(name="products", bufs=4))
 
+        bias_row = const.tile([1, FEATURES], BF16)
+        nc.sync.dma_start(out=bias_row[:, 0 : FEATURES // 2], in_=bq.unsqueeze(0))
+        nc.sync.dma_start(out=bias_row[:, FEATURES // 2 : FEATURES], in_=bk.unsqueeze(0))
         w_raw = const.tile([P, 4 * K], BF16)
         nc.sync.dma_start(
             out=w_raw[:, 0 : 2 * K].rearrange("p (c k) -> p c k", c=2), in_=Wq.rearrange("(c p) k -> p c k", p=P)
@@ -95,26 +94,27 @@ def tile_lorentzmultiheadattention_pa_t_kernel(tc, x_space, Wq, bq, Wk, bk, out_
 
         bias_rows = const.tile([P, FEATURES], BF16)
         nc.vector.memset(bias_rows[:], 0.0)
+        nc.vector.tensor_copy(out=bias_rows[0:1, :], in_=bias_row[:])
         ones = const.tile([P, P], BF16)
         nc.vector.memset(ones[:], 1.0)
-        nc.scalar.dma_start(out=bias_rows[0:1, 0 : FEATURES // 2], in_=bq.unsqueeze(0))
-        nc.scalar.dma_start(out=bias_rows[0:1, FEATURES // 2 : FEATURES], in_=bk.unsqueeze(0))
+        bias_bank = product_banks.tile([P, FEATURES], F32, tag="product")
+        nc.tensor.matmul(out=bias_bank[:], lhsT=ones[:], rhs=bias_rows[:], start=True, stop=True)
+        bias = const.tile([P, FEATURES], F32)
+        nc.vector.tensor_copy(out=bias[:], in_=bias_bank[:])
 
         w_grouped = const.tile([P, 4 * FEATURES], BF16, align_bytes=64)
         w_codes = const.tile([P, FEATURES], U32, align_bytes=64)
         w_scales = const.tile([P, FEATURES], U8, align_bytes=64)
         for j in range(2):
-            w_bank = transpose_two_tiles(
-                nc, turn_banks, identity[:], w_raw[:].bitcast(F32)[:, 2 * j * WORDS : 2 * (j + 1) * WORDS]
+            turn_two_tiles(
+                nc,
+                turn_banks,
+                identity[:],
+                w_raw[:].bitcast(F32)[:, 2 * j * WORDS : 2 * (j + 1) * WORDS],
+                w_grouped[:].bitcast(F32)[:, 4 * j * P : 4 * (j + 1) * P],
             )
-            regroup_two_tiles(nc.vector.tensor_copy, w_bank, w_grouped[:].bitcast(F32)[:, 4 * j * P : 4 * (j + 1) * P])
-        bias_bank = product_banks.tile([P, FEATURES], F32, tag="product")
-        nc.tensor.matmul(out=bias_bank[:], lhsT=ones[:], rhs=bias_rows[:], start=True, stop=True)
-        bias = const.tile([P, FEATURES], F32)
-        nc.vector.tensor_copy(out=bias[:], in_=bias_bank[:])
         nc.vector.quantize_mx(out=w_codes[:].bitcast(FP8X4), scales=w_scales[:], in_=w_grouped[:])
 
-        turned = {}
         grouped = {}
         codes = {}
         scales = {}
@@ -122,21 +122,16 @@ def tile_lorentzmultiheadattention_pa_t_kernel(tc, x_space, Wq, bq, Wk, bk, out_
         partial_sums = {}
         norms = {}
 
-        def transpose_batch(b):
-            for half_batch in (2 * b, 2 * b + 1):
-                turned[half_batch] = [
-                    transpose_two_tiles(
-                        nc, turn_banks, identity[:], x_words[half_batch][:, 2 * j * WORDS : 2 * (j + 1) * WORDS]
-                    )
-                    for j in range(HALF // 2)
-                ]
-
-        def regroup(half_batch):
+        def turn(half_batch):
             x_grouped = mx_pool.tile([P, 4 * HALF * P], BF16, align_bytes=64)
             grouped[half_batch] = x_grouped
             for j in range(HALF // 2):
-                regroup_two_tiles(
-                    nc.scalar.copy, turned[half_batch][j], x_grouped[:].bitcast(F32)[:, 4 * j * P : 4 * (j + 1) * P]
+                turn_two_tiles(
+                    nc,
+                    turn_banks,
+                    identity[:],
+                    x_words[half_batch][:, 2 * j * WORDS : 2 * (j + 1) * WORDS],
+                    x_grouped[:].bitcast(F32)[:, 4 * j * P : 4 * (j + 1) * P],
                 )
 
         def quantise(half_batch):
@@ -182,6 +177,9 @@ def tile_lorentzmultiheadattention_pa_t_kernel(tc, x_space, Wq, bq, Wk, bk, out_
         def square(piece):
             squares = sum_pool.tile([P, PIECE_ROWS, HEAD], F32)
             nc.scalar.activation(out=squares[:], in_=lifted[piece][:, :, 1:ROW], func=SQUARE)
+            partial_sums[piece] = squares
+            if piece >= PIECES - ROUND_PIECES:
+                return
             half_sums = sum_pool.tile([P, PIECE_ROWS, HEAD // 2], F32)
             nc.gpsimd.tensor_tensor(
                 out=half_sums[:], in0=squares[:, :, 0 : HEAD // 2], in1=squares[:, :, HEAD // 2 : HEAD], op=ADD
@@ -225,10 +223,8 @@ def tile_lorentzmultiheadattention_pa_t_kernel(tc, x_space, Wq, bq, Wk, bk, out_
                 quantise(r - LAG_QUANTISE)
             for piece in pieces_of(r - LAG_SQUARE):
                 square(piece)
-            if r < HALF_BATCHES and r % 2 == 0:
-                transpose_batch(r // 2)
             if r < HALF_BATCHES:
-                regroup(r)
+                turn(r)
             for piece in pieces_of(r - LAG_REDUCE):
                 reduce_rows(piece)
             for piece in pieces_of(r - LAG_ROOT):

from contextlib import ExitStack

import concourse.mybir as mybir
from concourse.masks import make_identity

F32 = mybir.dt.float32
BF16 = mybir.dt.bfloat16
U32 = mybir.dt.uint32
U8 = mybir.dt.uint8
FP8X4 = mybir.dt.float8_e4m3fn_x4
ADD = mybir.AluOpType.add
SQUARE = mybir.ActivationFunctionType.Square
SQRT = mybir.ActivationFunctionType.Sqrt

P = 128
BATCHES = 8
TOKENS = 1024
K = 512
WORDS = K // 2
FEATURES = 512
HEAD = 64
ROW = HEAD + 1
TILES = TOKENS // P
HALF = TILES // 2
PIECE_HEADS = P // HEAD
PIECE_ROWS = PIECE_HEADS * TILES
PIECES_PER_BATCH = FEATURES // P
PIECES = BATCHES * PIECES_PER_BATCH
HALF_BATCHES = 2 * BATCHES
ROUND_PIECES = PIECES // HALF_BATCHES

LAG_QUANTISE = 1
LAG_PROJECT = 3
LAG_SQUARE = LAG_PROJECT + 1
LAG_REDUCE = LAG_SQUARE + 1
LAG_ROOT = LAG_REDUCE + 1

SECOND_HALVING_EVERY = 2

FLOPS = 2 * BATCHES * TOKENS * K * FEATURES


def turn_two_tiles(nc, banks, identity, raw_words, grouped_words):
    bank = banks.tile([P, 4 * P], F32)
    for i in range(2):
        for u in range(2):
            nc.tensor.transpose(
                bank[:, (2 * i + u) * P : (2 * i + u + 1) * P],
                raw_words[:, i * WORDS + u * P : i * WORDS + (u + 1) * P],
                identity,
            )
    nc.scalar.copy(
        out=grouped_words.rearrange("p (i r u) -> p i r u", i=2, u=2),
        in_=bank[:].rearrange("p (i u r) -> p i r u", i=2, u=2),
    )


def tile_lorentzmultiheadattention_pa_t_kernel(tc, x_space, Wq, bq, Wk, bk, out_0, out_1):
    nc = tc.nc
    with ExitStack() as stack:
        stack.enter_context(tc.manual_schedule())
        const = stack.enter_context(tc.tile_pool(name="const", bufs=1))
        x_pool = stack.enter_context(tc.tile_pool(name="x", bufs=2 * BATCHES))
        mx_pool = stack.enter_context(tc.tile_pool(name="mx", bufs=4))
        out_pool = stack.enter_context(tc.tile_pool(name="lifted", bufs=12))
        sum_pool = stack.enter_context(tc.tile_pool(name="sums", bufs=4))
        turn_banks = stack.enter_context(tc.psum_pool(name="turned", bufs=4))
        product_banks = stack.enter_context(tc.psum_pool(name="products", bufs=4))

        bias_row = const.tile([1, FEATURES], BF16)
        nc.sync.dma_start(out=bias_row[:, 0 : FEATURES // 2], in_=bq.unsqueeze(0))
        nc.sync.dma_start(out=bias_row[:, FEATURES // 2 : FEATURES], in_=bk.unsqueeze(0))
        w_raw = const.tile([P, 4 * K], BF16)
        nc.sync.dma_start(
            out=w_raw[:, 0 : 2 * K].rearrange("p (c k) -> p c k", c=2), in_=Wq.rearrange("(c p) k -> p c k", p=P)
        )
        nc.sync.dma_start(
            out=w_raw[:, 2 * K : 4 * K].rearrange("p (c k) -> p c k", c=2), in_=Wk.rearrange("(c p) k -> p c k", p=P)
        )
        x_words = []
        for b in range(BATCHES):
            x_by_tile = x_space[b].rearrange("(p t) k -> p t k", t=TILES)
            for half in range(2):
                x_raw = x_pool.tile([P, HALF, K], BF16)
                nc.sync.dma_start(out=x_raw[:], in_=x_by_tile[:, half * HALF : (half + 1) * HALF, :])
                x_words.append(x_raw[:].rearrange("p t k -> p (t k)").bitcast(F32))

        identity = const.tile([P, P], F32)
        make_identity(nc, identity[:])
        one = const.tile([P, 1], F32)
        nc.vector.memset(one[:], 1.0)
        warm = const.tile([P, 1], F32)
        nc.scalar.activation(out=warm[:], in_=one[:], func=SQRT)

        bias_rows = const.tile([P, FEATURES], BF16)
        nc.vector.memset(bias_rows[:], 0.0)
        nc.vector.tensor_copy(out=bias_rows[0:1, :], in_=bias_row[:])
        ones = const.tile([P, P], BF16)
        nc.vector.memset(ones[:], 1.0)
        bias_bank = product_banks.tile([P, FEATURES], F32, tag="product")
        nc.tensor.matmul(out=bias_bank[:], lhsT=ones[:], rhs=bias_rows[:], start=True, stop=True)
        bias = const.tile([P, FEATURES], F32)
        nc.vector.tensor_copy(out=bias[:], in_=bias_bank[:])

        w_grouped = const.tile([P, 4 * FEATURES], BF16, align_bytes=64)
        w_codes = const.tile([P, FEATURES], U32, align_bytes=64)
        w_scales = const.tile([P, FEATURES], U8, align_bytes=64)
        for j in range(2):
            turn_two_tiles(
                nc,
                turn_banks,
                identity[:],
                w_raw[:].bitcast(F32)[:, 2 * j * WORDS : 2 * (j + 1) * WORDS],
                w_grouped[:].bitcast(F32)[:, 4 * j * P : 4 * (j + 1) * P],
            )
        nc.vector.quantize_mx(out=w_codes[:].bitcast(FP8X4), scales=w_scales[:], in_=w_grouped[:])

        grouped = {}
        codes = {}
        scales = {}
        lifted = {}
        partial_sums = {}
        norms = {}

        def turn(half_batch):
            x_grouped = mx_pool.tile([P, 4 * HALF * P], BF16, align_bytes=64)
            grouped[half_batch] = x_grouped
            for j in range(HALF // 2):
                turn_two_tiles(
                    nc,
                    turn_banks,
                    identity[:],
                    x_words[half_batch][:, 2 * j * WORDS : 2 * (j + 1) * WORDS],
                    x_grouped[:].bitcast(F32)[:, 4 * j * P : 4 * (j + 1) * P],
                )

        def quantise(half_batch):
            x_codes = mx_pool.tile([P, HALF * P], U32, align_bytes=64)
            x_scales = mx_pool.tile([P, HALF * P], U8, align_bytes=64)
            nc.vector.quantize_mx(out=x_codes[:].bitcast(FP8X4), scales=x_scales[:], in_=grouped[half_batch][:])
            codes[half_batch] = x_codes
            scales[half_batch] = x_scales

        def project(piece):
            b, c = divmod(piece, PIECES_PER_BATCH)
            features = slice(c * P, (c + 1) * P)
            rows = out_pool.tile([P, PIECE_ROWS, ROW], F32)
            lifted[piece] = rows
            u_by_tile = rows[:, :, 1:ROW].rearrange("p (h t) d -> p t h d", h=PIECE_HEADS)
            bias_by_tile = (
                bias[:, features]
                .rearrange("p (h d) -> p h d", h=PIECE_HEADS)
                .unsqueeze(1)
                .to_broadcast([P, HALF, PIECE_HEADS, HEAD])
            )
            for half in range(2):
                half_batch = 2 * b + half
                product = product_banks.tile([P, HALF * P], F32)
                for i in range(HALF):
                    tokens = slice(i * P, (i + 1) * P)
                    nc.tensor.matmul_mx(
                        out=product[:, tokens],
                        lhsT=codes[half_batch][:, tokens].bitcast(FP8X4),
                        lhsT_scale=scales[half_batch][:, tokens],
                        rhs=w_codes[:, features].bitcast(FP8X4),
                        rhs_scale=w_scales[:, features],
                        start=True,
                        stop=True,
                    )
                nc.vector.tensor_tensor(
                    out=u_by_tile[:, half * HALF : (half + 1) * HALF],
                    in0=product[:].rearrange("p (t h d) -> p t h d", t=HALF, h=PIECE_HEADS),
                    in1=bias_by_tile,
                    op=ADD,
                )

        def square(piece):
            squares = sum_pool.tile([P, PIECE_ROWS, HEAD], F32)
            nc.scalar.activation(out=squares[:], in_=lifted[piece][:, :, 1:ROW], func=SQUARE)
            partial_sums[piece] = squares
            if piece >= PIECES - ROUND_PIECES:
                return
            half_sums = sum_pool.tile([P, PIECE_ROWS, HEAD // 2], F32)
            nc.gpsimd.tensor_tensor(
                out=half_sums[:], in0=squares[:, :, 0 : HEAD // 2], in1=squares[:, :, HEAD // 2 : HEAD], op=ADD
            )
            partial_sums[piece] = half_sums
            if piece % SECOND_HALVING_EVERY == 0:
                quarter_sums = sum_pool.tile([P, PIECE_ROWS, HEAD // 4], F32)
                nc.gpsimd.tensor_tensor(
                    out=quarter_sums[:],
                    in0=half_sums[:, :, 0 : HEAD // 4],
                    in1=half_sums[:, :, HEAD // 4 : HEAD // 2],
                    op=ADD,
                )
                partial_sums[piece] = quarter_sums

        def reduce_rows(piece):
            norm = sum_pool.tile([P, PIECE_ROWS], F32)
            nc.vector.tensor_reduce(out=norm[:], in_=partial_sums[piece][:], axis=mybir.AxisListType.X, op=ADD)
            norms[piece] = norm

        def root_and_store(piece):
            b, c = divmod(piece, PIECES_PER_BATCH)
            rows = lifted[piece]
            nc.scalar.activation(out=rows[:, :, 0], in_=norms[piece][:], func=SQRT, bias=one[:])
            target = (out_0, out_1)[c // 2]
            first_head = PIECE_HEADS * (c % 2)
            nc.sync.dma_start(
                out=target[b, first_head : first_head + PIECE_HEADS].rearrange("h (p t) d -> p h (t d)", t=TILES),
                in_=rows[:].rearrange("p (h t) d -> p h (t d)", h=PIECE_HEADS),
            )

        def pieces_of(r):
            if 0 <= r < HALF_BATCHES:
                return range(ROUND_PIECES * r, ROUND_PIECES * (r + 1))
            return range(0)

        for r in range(HALF_BATCHES + LAG_ROOT):
            for piece in pieces_of(r - LAG_PROJECT):
                project(piece)
            if 0 <= r - LAG_QUANTISE < HALF_BATCHES:
                quantise(r - LAG_QUANTISE)
            for piece in pieces_of(r - LAG_SQUARE):
                square(piece)
            if r < HALF_BATCHES:
                turn(r)
            for piece in pieces_of(r - LAG_REDUCE):
                reduce_rows(piece)
            for piece in pieces_of(r - LAG_ROOT):
                root_and_store(piece)
